import numpy as np
import ml_dtypes


def mxq(x, axis, fmt="e4m3"):
    dtype, down = {"e4m3": (ml_dtypes.float8_e4m3fn, 7), "e5m2": (ml_dtypes.float8_e5m2, 14)}[fmt]
    v = np.moveaxis(np.asarray(x, np.float32).astype(ml_dtypes.bfloat16).astype(np.float64), axis, -1)
    blocks = v.reshape(v.shape[:-1] + (-1, 32))
    amax = np.abs(blocks).max(-1, keepdims=True)
    byte = np.maximum(np.where(amax > 0, np.frexp(amax)[1] - 1 + 127, 0) - down, 1)
    scale = np.exp2(byte - 127.0)
    codes = (blocks / scale).astype(np.float32).astype(dtype).astype(np.float64)
    return np.moveaxis((codes * scale).reshape(v.shape), -1, axis)


WIDE = False


def mx_kscale(k):
    if not WIDE:
        return np.ones(k)
    levels = np.array([10, -10, 5, -5, 0])
    if k % 512:
        return np.exp2(np.random.permutation(np.resize(levels, k // 32))).repeat(32)
    a = np.empty((k // 512, 16))
    for p in range(k // 512):
        a[p, :8] = np.random.permutation(np.resize(levels, 8))
        for g in range(8):
            far = levels[np.abs(levels - a[p, g]) >= 10]
            a[p, g + 8] = far[np.random.randint(len(far))]
    return np.exp2(a.ravel()).repeat(32)


BF16 = ml_dtypes.bfloat16


def bf(x):
    return np.asarray(x, np.float32).astype(BF16)


def f64(x):
    return np.asarray(x).astype(np.float64)


N, C = 768, 512
KV = 2 * C
SQRT2 = np.sqrt(2.0)
EPS = 1e-6


def setup_inputs():
    t = mx_kscale(KV)
    return {"s": bf(np.random.standard_normal((N, C))),
            "v": bf(np.random.standard_normal((N, C, 3))),
            "g_v": bf(np.random.standard_normal((N, KV)) * t),
            "wv": bf(np.random.standard_normal((KV, C)) / t[:, None]),
            "ln_g1": bf(1.0 + 0.1 * np.random.standard_normal(C))}


def reference(s, v, g_v, wv, ln_g1):
    s, v = f64(s), f64(v)
    sv = SQRT2 * s[..., None] * v
    vec = np.concatenate([v, sv], axis=1) * f64(g_v)[..., None]
    dv = (mxq(vec.transpose(0, 2, 1), 2, "e4m3") @ mxq(f64(wv), 0, "e4m3")) / np.sqrt(KV)
    y = v + dv.transpose(0, 2, 1)
    rms = np.sqrt(np.mean(y * y, axis=(1, 2), keepdims=True) + EPS)
    return y / rms * f64(ln_g1)[None, :, None]

@@ -1,0 +1,246 @@
+from contextlib import ExitStack
+import math
+
+import concourse.mybir as mybir
+from concourse.masks import make_identity
+
+BF16 = mybir.dt.bfloat16
+F32 = mybir.dt.float32
+U32 = mybir.dt.uint32
+U8 = mybir.dt.uint8
+FP8X4 = mybir.dt.float8_e4m3fn_x4
+MULT = mybir.AluOpType.mult
+ADD = mybir.AluOpType.add
+ACT = mybir.ActivationFunctionType
+
+P = 128
+PACK = 4
+POINTS = 768
+C = 512
+DIMS = 3
+PASSES = 2
+TILES = POINTS // P
+EPS = 1e-6
+GROUPS = ((0,), (1, 2))
+
+FLOPS = 2 * POINTS * DIMS * (PASSES * C) * C
+
+
+def tile_selfinteraction_pb_kernel(tc, s, v, g_v, wv, ln_g1, out):
+    nc = tc.nc
+    with ExitStack() as ctx:
+        const = ctx.enter_context(tc.tile_pool(name="const", bufs=1))
+        resident = ctx.enter_context(tc.tile_pool(name="resident", bufs=1))
+        work = ctx.enter_context(tc.tile_pool(name="work", bufs=2))
+        psum_t = ctx.enter_context(tc.psum_pool(name="psum_t", bufs=1))
+        psum_acc = ctx.enter_context(tc.psum_pool(name="psum_acc", bufs=4))
+        ctx.enter_context(tc.manual_schedule())
+
+        g_sb = [resident.tile([P, PASSES, P, PACK], BF16, name="g_sb%d" % i) for i in range(TILES)]
+        s_sb = [resident.tile([P, P, PACK], BF16, name="s_sb%d" % i) for i in range(TILES)]
+        v_sb = [resident.tile([P, C, DIMS], BF16, name="v_sb%d" % i) for i in range(TILES)]
+        wv_sb = [resident.tile([P, PACK, C], BF16, name="wv_sb%d" % h) for h in range(PASSES)]
+        gain = const.tile([P, C], BF16)
+
+        def load_point_tile(i):
+            rows = slice(i * P, (i + 1) * P)
+            nc.sync.dma_start(out=g_sb[i][:], in_=g_v[rows, :].rearrange("n (h m t) -> n h m t", t=PACK, m=P))
+            nc.sync.dma_start(out=v_sb[i][:], in_=v[rows, :, :])
+            nc.sync.dma_start(out=s_sb[i][:], in_=s[rows, :].rearrange("n (m t) -> n m t", m=P))
+
+        load_point_tile(0)
+        for h in range(PASSES):
+            nc.sync.dma_start(
+                out=wv_sb[h][:],
+                in_=wv[h * PACK * P : (h + 1) * PACK * P, :].rearrange("(p t) c -> p t c", t=PACK),
+            )
+        nc.sync.dma_start(out=gain[:], in_=ln_g1.partition_broadcast(P))
+        for i in range(1, TILES):
+            load_point_tile(i)
+
+        ident_bf16 = const.tile([P, P], BF16)
+        make_identity(nc, ident_bf16[:])
+        ident_f32 = const.tile([P, P], F32)
+        make_identity(nc, ident_f32[:])
+        one = const.tile([P, 1], F32)
+        nc.vector.memset(one[:], 1.0)
+        nc.scalar.activation(out=one[:], in_=one[:], func=ACT.Abs_reciprocal_sqrt)
+
+        wv_grouped = const.tile([P, PASSES, C, PACK], BF16, align_bytes=64)
+        wv_codes = const.tile([P, PASSES, C], U32, align_bytes=64)
+        wv_scales = const.tile([P, PASSES, C], U8, align_bytes=64)
+
+        def group_wv(h):
+            dst = wv_grouped[:, h].rearrange("p (c i) t -> p c t i", i=4)
+            src = wv_sb[h][:].rearrange("p t (c i) -> p c t i", i=4)
+            if h == 0:
+                nc.scalar.copy(out=dst, in_=src)
+            else:
+                nc.gpsimd.tensor_scalar(out=dst, in0=src, scalar1=1.0, scalar2=0.0, op0=MULT, op1=ADD)
+
+        def quantise_wv(h):
+            nc.vector.quantize_mx(
+                out=wv_codes[:, h, :].bitcast(FP8X4),
+                scales=wv_scales[:, h, :],
+                in_=wv_grouped[:, h].rearrange("p c t -> p (c t)"),
+            )
+
+        sg_nat, g1T_ps, sgT_ps, g1T, sgT, vT_ps = {}, {}, {}, {}, {}, {}
+        u, u_codes, u_scales = {}, {}, {}
+        acc, y, y_gain, mean_sq, inv_rms = {}, {}, {}, {}, {}
+
+        def second_gate(i):
+            sg_nat[i] = resident.tile([P, P, PACK], F32, name="sg_nat%d" % i)
+            nc.gpsimd.tensor_tensor(out=sg_nat[i][:], in0=s_sb[i][:], in1=g_sb[i][:, 1], op=MULT)
+
+        def transpose_first_gate(i):
+            g1T_ps[i] = psum_t.tile([P, PACK, P], BF16, name="g1T_ps", tag="g1T_ps")
+            for t in range(PACK):
+                nc.tensor.transpose(g1T_ps[i][:, t, :], g_sb[i][:, 0, :, t], ident_bf16[:])
+
+        def transpose_second_gate(i):
+            sgT_ps[i] = psum_t.tile([P, PACK, P], F32, name="sgT_ps", tag="sgT_ps")
+            for t in range(PACK):
+                nc.tensor.transpose(sgT_ps[i][:, t, :], sg_nat[i][:, :, t], ident_f32[:])
+
+        def copy_first_gate(i):
+            g1T[i] = work.tile([P, P, PACK], BF16, name="g1T", tag="g1T")
+            nc.scalar.copy(out=g1T[i][:], in_=g1T_ps[i][:].rearrange("p t n -> p n t"))
+
+        def copy_second_gate(i):
+            sgT[i] = work.tile([P, P, PACK], F32, name="sgT", tag="sgT")
+            nc.scalar.mul(out=sgT[i][:], in_=sgT_ps[i][:].rearrange("p t n -> p n t"), mul=math.sqrt(2.0))
+
+        def transpose_v(i, k):
+            vT_ps[i, k] = psum_t.tile([P, len(GROUPS[k]), PACK, P], BF16, name="vT_ps%d" % k, tag="vT_ps%d" % k)
+            for e, d in enumerate(GROUPS[k]):
+                for t in range(PACK):
+                    nc.tensor.transpose(vT_ps[i, k][:, e, t, :], v_sb[i][:, t:C:PACK, d], ident_bf16[:])
+
+        def product(i, k, h, gate):
+            if h == 0:
+                u[i, k] = work.tile(
+                    [P, PASSES, len(GROUPS[k]), P, PACK], BF16, name="u%d" % k, tag="u%d" % k, align_bytes=64
+                )
+            nc.vector.tensor_tensor(
+                out=u[i, k][:, h],
+                in0=vT_ps[i, k][:].rearrange("p e t n -> p e n t"),
+                in1=gate[:].unsqueeze(1).to_broadcast([P, len(GROUPS[k]), P, PACK]),
+                op=MULT,
+            )
+
+        def quantise(i, k):
+            shape = [P, PASSES, len(GROUPS[k]), P]
+            u_codes[i, k] = work.tile(shape, U32, name="u_codes%d" % k, tag="u_codes%d" % k, align_bytes=64)
+            u_scales[i, k] = work.tile(shape, U8, name="u_scales%d" % k, tag="u_scales%d" % k, align_bytes=64)
+            nc.vector.quantize_mx(
+                out=u_codes[i, k][:].rearrange("p h e n -> p (h e n)").bitcast(FP8X4),
+                scales=u_scales[i, k][:].rearrange("p h e n -> p (h e n)"),
+                in_=u[i, k][:].rearrange("p h e n t -> p (h e n t)"),
+            )
+
+        def multiply(i, k):
+            for e, d in enumerate(GROUPS[k]):
+                acc[i, d] = psum_acc.tile([P, C], F32, name="acc", tag="acc")
+                for h in range(PASSES):
+                    nc.tensor.matmul_mx(
+                        out=acc[i, d][:],
+                        lhsT=u_codes[i, k][:, h, e, :].bitcast(FP8X4),
+                        lhsT_scale=u_scales[i, k][:, h, e, :],
+                        rhs=wv_codes[:, h, :].bitcast(FP8X4),
+                        rhs_scale=wv_scales[:, h, :],
+                        start=(h == 0),
+                        stop=(h == PASSES - 1),
+                    )
+
+        def residual(i, d):
+            if d == 0:
+                y[i] = work.tile([P, DIMS, C], F32, name="y", tag="y")
+                y_gain[i] = work.tile([P, DIMS, C], F32, name="y_gain", tag="y_gain")
+            nc.vector.scalar_tensor_tensor(
+                out=y[i][:, d, :], in0=acc[i, d][:], scalar=1.0 / math.sqrt(PASSES * C),
+                in1=v_sb[i][:, :, d], op0=MULT, op1=ADD,
+            )
+            nc.gpsimd.tensor_tensor(out=y_gain[i][:, d, :], in0=y[i][:, d, :], in1=gain[:], op=MULT)
+
+        def mean_square(i, first, last):
+            squares = work.tile([P, DIMS, C], F32, name="squares", tag="squares")
+            share = work.tile([P, 1], F32, name="share", tag="share", bufs=4)
+            nc.scalar.activation(
+                out=squares[:, first:last, :], in_=y[i][:, first:last, :], func=ACT.Square,
+                scale=1.0 / math.sqrt(DIMS * C), accum_out=share[:],
+            )
+            return share
+
+        def mean_square_of_two(i):
+            share = mean_square(i, 0, 2)
+            mean_sq[i] = work.tile([P, 1], F32, name="mean_sq", tag="mean_sq")
+            nc.scalar.activation(out=mean_sq[i][:], in_=share[:], func=ACT.Copy, bias=EPS)
+
+        def inverse_rms(i):
+            share = mean_square(i, 2, DIMS)
+            inv_rms[i] = work.tile([P, 1], F32, name="inv_rms", tag="inv_rms")
+            nc.scalar.activation(
+                out=inv_rms[i][:], in_=share[:], func=ACT.Abs_reciprocal_sqrt, bias=mean_sq[i][:]
+            )
+
+        def normalise_and_store(i):
+            for half in range(2):
+                cols = slice(half * C // 2, (half + 1) * C // 2)
+                result = work.tile([P, C // 2, DIMS], F32, name="result", tag="result", bufs=4)
+                nc.scalar.activation(
+                    out=result[:], in_=y_gain[i][:, :, cols].rearrange("p d c -> p c d"),
+                    func=ACT.Copy, scale=inv_rms[i][:],
+                )
+                nc.sync.dma_start(out=out[i * P : (i + 1) * P, cols, :], in_=result[:])
+
+        second_gate(0)
+        transpose_first_gate(0)
+        copy_first_gate(0)
+        transpose_v(0, 0)
+        transpose_v(0, 1)
+        transpose_second_gate(0)
+        copy_second_gate(0)
+        for h in range(PASSES):
+            group_wv(h)
+        for i in range(1, TILES):
+            second_gate(i)
+
+        for j in range(TILES + 2):
+            forming = j < TILES
+            preparing = j + 1 < TILES
+            adding = 0 <= j - 1 < TILES
+            storing = 0 <= j - 2
+            if preparing:
+                transpose_first_gate(j + 1)
+                transpose_second_gate(j + 1)
+                copy_first_gate(j + 1)
+                copy_second_gate(j + 1)
+            if storing:
+                normalise_and_store(j - 2)
+            if forming:
+                product(j, 0, 0, g1T[j])
+                product(j, 1, 0, g1T[j])
+                product(j, 0, 1, sgT[j])
+            if preparing:
+                transpose_v(j + 1, 0)
+            if forming:
+                product(j, 1, 1, sgT[j])
+            if preparing:
+                transpose_v(j + 1, 1)
+            if forming:
+                quantise(j, 0)
+                if j == 0:
+                    for h in range(PASSES):
+                        quantise_wv(h)
+                quantise(j, 1)
+                multiply(j, 0)
+            if adding:
+                residual(j - 1, 0)
+                residual(j - 1, 1)
+                mean_square_of_two(j - 1)
+            if forming:
+                multiply(j, 1)
+            if adding:
+                residual(j - 1, 2)
+                inverse_rms(j - 1)

@@ -45,18 +45,22 @@ def tile_selfinteraction_pb_kernel(tc, s, v, g_v, wv, ln_g1, out):
         def load_point_tile(i):
             rows = slice(i * P, (i + 1) * P)
             nc.sync.dma_start(out=g_sb[i][:], in_=g_v[rows, :].rearrange("n (h m t) -> n h m t", t=PACK, m=P))
-            nc.sync.dma_start(out=v_sb[i][:], in_=v[rows, :, :])
             nc.sync.dma_start(out=s_sb[i][:], in_=s[rows, :].rearrange("n (m t) -> n m t", m=P))
+            nc.sync.dma_start(out=v_sb[i][:], in_=v[rows, :, :])
 
-        load_point_tile(0)
-        for h in range(PASSES):
+        def load_wv(h):
             nc.sync.dma_start(
                 out=wv_sb[h][:],
                 in_=wv[h * PACK * P : (h + 1) * PACK * P, :].rearrange("(p t) c -> p t c", t=PACK),
             )
-        nc.sync.dma_start(out=gain[:], in_=ln_g1.partition_broadcast(P))
-        for i in range(1, TILES):
+        load_point_tile(0)
+        load_wv(0)
+        load_point_tile(1)
+        load_wv(1)
+        for i in range(2, TILES):
             load_point_tile(i)
+            if i == 2:
+                nc.sync.dma_start(out=gain[:], in_=ln_g1.partition_broadcast(P))
 
         ident_bf16 = const.tile([P, P], BF16)
         make_identity(nc, ident_bf16[:])
@@ -65,6 +69,8 @@ def tile_selfinteraction_pb_kernel(tc, s, v, g_v, wv, ln_g1, out):
         one = const.tile([P, 1], F32)
         nc.vector.memset(one[:], 1.0)
         nc.scalar.activation(out=one[:], in_=one[:], func=ACT.Abs_reciprocal_sqrt)
+        eps = const.tile([P, 1], F32)
+        nc.scalar.activation(out=eps[:], in_=one[:], func=ACT.Copy, scale=0.0, bias=EPS)
 
         wv_grouped = const.tile([P, PASSES, C, PACK], BF16, align_bytes=64)
         wv_codes = const.tile([P, PASSES, C], U32, align_bytes=64)
@@ -73,10 +79,7 @@ def tile_selfinteraction_pb_kernel(tc, s, v, g_v, wv, ln_g1, out):
         def group_wv(h):
             dst = wv_grouped[:, h].rearrange("p (c i) t -> p c t i", i=4)
             src = wv_sb[h][:].rearrange("p t (c i) -> p c t i", i=4)
-            if h == 0:
-                nc.scalar.copy(out=dst, in_=src)
-            else:
-                nc.gpsimd.tensor_scalar(out=dst, in0=src, scalar1=1.0, scalar2=0.0, op0=MULT, op1=ADD)
+            nc.scalar.copy(out=dst, in_=src)
 
         def quantise_wv(h):
             nc.vector.quantize_mx(
@@ -89,9 +92,9 @@ def tile_selfinteraction_pb_kernel(tc, s, v, g_v, wv, ln_g1, out):
         u, u_codes, u_scales = {}, {}, {}
         acc, y, y_gain, mean_sq, inv_rms = {}, {}, {}, {}, {}
 
-        def second_gate(i):
+        def second_gate(i, engine):
             sg_nat[i] = resident.tile([P, P, PACK], F32, name="sg_nat%d" % i)
-            nc.gpsimd.tensor_tensor(out=sg_nat[i][:], in0=s_sb[i][:], in1=g_sb[i][:, 1], op=MULT)
+            engine.tensor_tensor(out=sg_nat[i][:], in0=s_sb[i][:], in1=g_sb[i][:, 1], op=MULT)
 
         def transpose_first_gate(i):
             g1T_ps[i] = psum_t.tile([P, PACK, P], BF16, name="g1T_ps", tag="g1T_ps")
@@ -155,13 +158,18 @@ def tile_selfinteraction_pb_kernel(tc, s, v, g_v, wv, ln_g1, out):
 
         def residual(i, d):
             if d == 0:
-                y[i] = work.tile([P, DIMS, C], F32, name="y", tag="y")
-                y_gain[i] = work.tile([P, DIMS, C], F32, name="y_gain", tag="y_gain")
+                y[i] = work.tile([P, DIMS, C], F32, name="y", tag="y", bufs=3)
             nc.vector.scalar_tensor_tensor(
                 out=y[i][:, d, :], in0=acc[i, d][:], scalar=1.0 / math.sqrt(PASSES * C),
                 in1=v_sb[i][:, :, d], op0=MULT, op1=ADD,
             )
-            nc.gpsimd.tensor_tensor(out=y_gain[i][:, d, :], in0=y[i][:, d, :], in1=gain[:], op=MULT)
+
+        def times_gain(i, d, cols):
+            if d == 0:
+                y_gain[i] = work.tile([P, DIMS, C], F32, name="y_gain", tag="y_gain")
+            nc.gpsimd.tensor_tensor(
+                out=y_gain[i][:, d, cols], in0=y[i][:, d, cols], in1=gain[:, cols], op=MULT
+            )
 
         def mean_square(i, first, last):
             squares = work.tile([P, DIMS, C], F32, name="squares", tag="squares")
@@ -172,75 +180,90 @@ def tile_selfinteraction_pb_kernel(tc, s, v, g_v, wv, ln_g1, out):
             )
             return share
 
-        def mean_square_of_two(i):
-            share = mean_square(i, 0, 2)
-            mean_sq[i] = work.tile([P, 1], F32, name="mean_sq", tag="mean_sq")
-            nc.scalar.activation(out=mean_sq[i][:], in_=share[:], func=ACT.Copy, bias=EPS)
+        def inverse_rms(i, share, bias):
+            inv_rms[i] = work.tile([P, 1], F32, name="inv_rms", tag="inv_rms", bufs=4)
+            nc.scalar.activation(out=inv_rms[i][:], in_=share[:], func=ACT.Abs_reciprocal_sqrt, bias=bias[:])
 
-        def inverse_rms(i):
-            share = mean_square(i, 2, DIMS)
-            inv_rms[i] = work.tile([P, 1], F32, name="inv_rms", tag="inv_rms")
+        def store(i, cols, result):
+            nc.sync.dma_start(out=out[i * P : (i + 1) * P, cols, :], in_=result[:])
+
+        def new_result():
+            return work.tile([P, C // 2, DIMS], F32, name="result", tag="result", bufs=4)
+
+        def normalise_on_scalar(i, cols):
+            result = new_result()
             nc.scalar.activation(
-                out=inv_rms[i][:], in_=share[:], func=ACT.Abs_reciprocal_sqrt, bias=mean_sq[i][:]
+                out=result[:], in_=y_gain[i][:, :, cols].rearrange("p d c -> p c d"),
+                func=ACT.Copy, scale=inv_rms[i][:],
             )
+            store(i, cols, result)
 
-        def normalise_and_store(i):
-            for half in range(2):
-                cols = slice(half * C // 2, (half + 1) * C // 2)
-                result = work.tile([P, C // 2, DIMS], F32, name="result", tag="result", bufs=4)
-                nc.scalar.activation(
-                    out=result[:], in_=y_gain[i][:, :, cols].rearrange("p d c -> p c d"),
-                    func=ACT.Copy, scale=inv_rms[i][:],
-                )
-                nc.sync.dma_start(out=out[i * P : (i + 1) * P, cols, :], in_=result[:])
+        def normalise_on_vector(i, cols):
+            result = new_result()
+            nc.vector.scalar_tensor_tensor(
+                out=result[:], in0=y[i][:, :, cols].rearrange("p d c -> p c d"), scalar=inv_rms[i][:],
+                in1=gain[:, cols].unsqueeze(2).to_broadcast([P, C // 2, DIMS]), op0=MULT, op1=MULT,
+            )
+            store(i, cols, result)
 
-        second_gate(0)
+        halves = [slice(half * C // 2, (half + 1) * C // 2) for half in range(2)]
+        everything = slice(0, C)
+
+        second_gate(0, nc.vector)
         transpose_first_gate(0)
         copy_first_gate(0)
         transpose_v(0, 0)
         transpose_v(0, 1)
         transpose_second_gate(0)
         copy_second_gate(0)
-        for h in range(PASSES):
-            group_wv(h)
+        group_wv(0)
         for i in range(1, TILES):
-            second_gate(i)
+            second_gate(i, nc.gpsimd)
 
-        for j in range(TILES + 2):
-            forming = j < TILES
-            preparing = j + 1 < TILES
-            adding = 0 <= j - 1 < TILES
-            storing = 0 <= j - 2
-            if preparing:
+        last = TILES - 1
+        for j in range(TILES):
+            if j < last:
                 transpose_first_gate(j + 1)
                 transpose_second_gate(j + 1)
                 copy_first_gate(j + 1)
                 copy_second_gate(j + 1)
-            if storing:
-                normalise_and_store(j - 2)
-            if forming:
-                product(j, 0, 0, g1T[j])
-                product(j, 1, 0, g1T[j])
-                product(j, 0, 1, sgT[j])
-            if preparing:
+            if j == 0:
+                group_wv(1)
+            if j >= 2:
+                for cols in halves:
+                    normalise_on_scalar(j - 2, cols)
+            product(j, 0, 0, g1T[j])
+            product(j, 1, 0, g1T[j])
+            product(j, 0, 1, sgT[j])
+            if j < last:
                 transpose_v(j + 1, 0)
-            if forming:
-                product(j, 1, 1, sgT[j])
-            if preparing:
+            product(j, 1, 1, sgT[j])
+            if j < last:
                 transpose_v(j + 1, 1)
-            if forming:
-                quantise(j, 0)
-                if j == 0:
-                    for h in range(PASSES):
-                        quantise_wv(h)
-                quantise(j, 1)
+            if j == 1:
+                for h in range(PASSES):
+                    quantise_wv(h)
+                multiply(0, 0)
+                multiply(0, 1)
+            quantise(j, 0)
+            quantise(j, 1)
+            if j >= 1:
                 multiply(j, 0)
-            if adding:
-                residual(j - 1, 0)
-                residual(j - 1, 1)
-                mean_square_of_two(j - 1)
-            if forming:
+                for d in range(DIMS):
+                    residual(j - 1, d)
+                    if j < last:
+                        times_gain(j - 1, d, everything)
                 multiply(j, 1)
-            if adding:
-                residual(j - 1, 2)
-                inverse_rms(j - 1)
+                inverse_rms(j - 1, mean_square(j - 1, 0, DIMS), eps)
+
+        for d in range(DIMS):
+            residual(last, d)
+            times_gain(last, d, halves[0])
+        share = mean_square(last, 0, 2)
+        mean_sq[last] = work.tile([P, 1], F32, name="mean_sq", tag="mean_sq")
+        nc.scalar.activation(out=mean_sq[last][:], in_=share[:], func=ACT.Copy, bias=EPS)
+        inverse_rms(last, mean_square(last, 2, DIMS), mean_sq[last])
+        for cols in halves:
+            normalise_on_vector(last - 1, cols)
+        normalise_on_scalar(last, halves[0])
+        normalise_on_vector(last, halves[1])

@@ -42,26 +42,38 @@ def tile_selfinteraction_pb_kernel(tc, s, v, g_v, wv, ln_g1, out):
         wv_sb = [resident.tile([P, PACK, C], BF16, name="wv_sb%d" % h) for h in range(PASSES)]
         gain = const.tile([P, C], BF16)
 
-        def load_point_tile(i):
+        def load_gate(i, h):
             rows = slice(i * P, (i + 1) * P)
-            nc.sync.dma_start(out=g_sb[i][:], in_=g_v[rows, :].rearrange("n (h m t) -> n h m t", t=PACK, m=P))
-            nc.sync.dma_start(out=s_sb[i][:], in_=s[rows, :].rearrange("n (m t) -> n m t", m=P))
-            nc.sync.dma_start(out=v_sb[i][:], in_=v[rows, :, :])
+            nc.sync.dma_start(
+                out=g_sb[i][:, h], in_=g_v[rows, h * C : (h + 1) * C].rearrange("n (m t) -> n m t", t=PACK)
+            )
+
+        def load_second_gate(i):
+            load_gate(i, 1)
+            nc.sync.dma_start(out=s_sb[i][:], in_=s[i * P : (i + 1) * P, :].rearrange("n (m t) -> n m t", t=PACK))
+
+        def load_rest(i):
+            load_gate(i, 0)
+            nc.sync.dma_start(out=v_sb[i][:], in_=v[i * P : (i + 1) * P, :, :])
 
         def load_wv(h):
             nc.sync.dma_start(
                 out=wv_sb[h][:],
                 in_=wv[h * PACK * P : (h + 1) * PACK * P, :].rearrange("(p t) c -> p t c", t=PACK),
             )
-        load_point_tile(0)
-        load_wv(0)
-        load_point_tile(1)
-        load_wv(1)
+        load_second_gate(0)
+        load_rest(0)
+        for i in range(1, TILES):
+            load_second_gate(i)
+        load_rest(1)
+        for h in range(PASSES):
+            load_wv(h)
+        nc.sync.dma_start(out=gain[:], in_=ln_g1.partition_broadcast(P))
         for i in range(2, TILES):
-            load_point_tile(i)
-            if i == 2:
-                nc.sync.dma_start(out=gain[:], in_=ln_g1.partition_broadcast(P))
+            load_rest(i)
 
+        warm = const.tile([P, C], BF16)
+        nc.vector.memset(warm[:], 0.0)
         ident_bf16 = const.tile([P, P], BF16)
         make_identity(nc, ident_bf16[:])
         ident_f32 = const.tile([P, P], F32)
@@ -88,18 +100,25 @@ def tile_selfinteraction_pb_kernel(tc, s, v, g_v, wv, ln_g1, out):
                 in_=wv_grouped[:, h].rearrange("p c t -> p (c t)"),
             )
 
+        last = TILES - 1
         sg_nat, g1T_ps, sgT_ps, g1T, sgT, vT_ps = {}, {}, {}, {}, {}, {}
         u, u_codes, u_scales = {}, {}, {}
         acc, y, y_gain, mean_sq, inv_rms = {}, {}, {}, {}, {}
+
+        def warm_up(i, matmuls):
+            spare = psum_t.tile([P, C], F32, name="warm_ps", tag="sgT_ps")
+            for k in range(matmuls):
+                nc.tensor.matmul(spare[:], lhsT=warm[:, 0:P], rhs=warm[:], start=True, stop=True)
 
         def second_gate(i, engine):
             sg_nat[i] = resident.tile([P, P, PACK], F32, name="sg_nat%d" % i)
             engine.tensor_tensor(out=sg_nat[i][:], in0=s_sb[i][:], in1=g_sb[i][:, 1], op=MULT)
 
         def transpose_first_gate(i):
-            g1T_ps[i] = psum_t.tile([P, PACK, P], BF16, name="g1T_ps", tag="g1T_ps")
-            for t in range(PACK):
-                nc.tensor.transpose(g1T_ps[i][:, t, :], g_sb[i][:, 0, :, t], ident_bf16[:])
+            g1T_ps[i] = psum_t.tile([P, PACK // 2, P], F32, name="g1T_ps", tag="g1T_ps")
+            words = g_sb[i][:, 0].bitcast(F32)
+            for w in range(PACK // 2):
+                nc.tensor.transpose(g1T_ps[i][:, w, :], words[:, :, w], ident_f32[:])
 
         def transpose_second_gate(i):
             sgT_ps[i] = psum_t.tile([P, PACK, P], F32, name="sgT_ps", tag="sgT_ps")
@@ -108,7 +127,7 @@ def tile_selfinteraction_pb_kernel(tc, s, v, g_v, wv, ln_g1, out):
 
         def copy_first_gate(i):
             g1T[i] = work.tile([P, P, PACK], BF16, name="g1T", tag="g1T")
-            nc.scalar.copy(out=g1T[i][:], in_=g1T_ps[i][:].rearrange("p t n -> p n t"))
+            nc.scalar.copy(out=g1T[i][:].bitcast(F32), in_=g1T_ps[i][:].rearrange("p w n -> p n w"))
 
         def copy_second_gate(i):
             sgT[i] = work.tile([P, P, PACK], F32, name="sgT", tag="sgT")
@@ -144,7 +163,10 @@ def tile_selfinteraction_pb_kernel(tc, s, v, g_v, wv, ln_g1, out):
 
         def multiply(i, k):
             for e, d in enumerate(GROUPS[k]):
-                acc[i, d] = psum_acc.tile([P, C], F32, name="acc", tag="acc")
+                if i == last and d > 0:
+                    acc[i, d] = psum_t.tile([P, C], F32, name="acc", tag="vT_ps%d" % (d - 1))
+                else:
+                    acc[i, d] = psum_acc.tile([P, C], F32, name="acc", tag="acc")
                 for h in range(PASSES):
                     nc.tensor.matmul_mx(
                         out=acc[i, d][:],
@@ -185,30 +207,33 @@ def tile_selfinteraction_pb_kernel(tc, s, v, g_v, wv, ln_g1, out):
             nc.scalar.activation(out=inv_rms[i][:], in_=share[:], func=ACT.Abs_reciprocal_sqrt, bias=bias[:])
 
         def store(i, cols, result):
-            nc.sync.dma_start(out=out[i * P : (i + 1) * P, cols, :], in_=result[:])
+            nc.sync.dma_start(out=out[i * P : (i + 1) * P, cols, :], in_=result)
 
-        def new_result():
-            return work.tile([P, C // 2, DIMS], F32, name="result", tag="result", bufs=4)
+        def new_result(cols):
+            tile = work.tile([P, C, DIMS], F32, name="result", tag="result", bufs=4)
+            return tile[:, 0 : cols.stop - cols.start, :]
 
         def normalise_on_scalar(i, cols):
-            result = new_result()
+            result = new_result(cols)
             nc.scalar.activation(
-                out=result[:], in_=y_gain[i][:, :, cols].rearrange("p d c -> p c d"),
+                out=result, in_=y_gain[i][:, :, cols].rearrange("p d c -> p c d"),
                 func=ACT.Copy, scale=inv_rms[i][:],
             )
             store(i, cols, result)
 
         def normalise_on_vector(i, cols):
-            result = new_result()
+            result = new_result(cols)
             nc.vector.scalar_tensor_tensor(
-                out=result[:], in0=y[i][:, :, cols].rearrange("p d c -> p c d"), scalar=inv_rms[i][:],
-                in1=gain[:, cols].unsqueeze(2).to_broadcast([P, C // 2, DIMS]), op0=MULT, op1=MULT,
+                out=result, in0=y[i][:, :, cols].rearrange("p d c -> p c d"), scalar=inv_rms[i][:],
+                in1=gain[:, cols].unsqueeze(2).to_broadcast([P, cols.stop - cols.start, DIMS]), op0=MULT, op1=MULT,
             )
             store(i, cols, result)
 
-        halves = [slice(half * C // 2, (half + 1) * C // 2) for half in range(2)]
         everything = slice(0, C)
+        scalar_cols = {last - 1: slice(0, C // 2), last: slice(0, C // 4)}
+        vector_cols = {i: slice(cols.stop, C) for i, cols in scalar_cols.items()}
 
+        warm_up(0, 4)
         second_gate(0, nc.vector)
         transpose_first_gate(0)
         copy_first_gate(0)
@@ -216,22 +241,22 @@ def tile_selfinteraction_pb_kernel(tc, s, v, g_v, wv, ln_g1, out):
         transpose_v(0, 1)
         transpose_second_gate(0)
         copy_second_gate(0)
-        group_wv(0)
         for i in range(1, TILES):
             second_gate(i, nc.gpsimd)
 
-        last = TILES - 1
         for j in range(TILES):
             if j < last:
                 transpose_first_gate(j + 1)
                 transpose_second_gate(j + 1)
                 copy_first_gate(j + 1)
                 copy_second_gate(j + 1)
+            if j == last:
+                warm_up(j, 4)
             if j == 0:
-                group_wv(1)
+                for h in range(PASSES):
+                    group_wv(h)
             if j >= 2:
-                for cols in halves:
-                    normalise_on_scalar(j - 2, cols)
+                normalise_on_scalar(j - 2, everything)
             product(j, 0, 0, g1T[j])
             product(j, 1, 0, g1T[j])
             product(j, 0, 1, sgT[j])
@@ -241,29 +266,45 @@ def tile_selfinteraction_pb_kernel(tc, s, v, g_v, wv, ln_g1, out):
             if j < last:
                 transpose_v(j + 1, 1)
             if j == 1:
+                quantise(0, 0)
+                quantise(0, 1)
                 for h in range(PASSES):
                     quantise_wv(h)
                 multiply(0, 0)
                 multiply(0, 1)
-            quantise(j, 0)
-            quantise(j, 1)
+            if j >= 1:
+                quantise(j, 0)
+                quantise(j, 1)
             if j >= 1:
                 multiply(j, 0)
                 for d in range(DIMS):
                     residual(j - 1, d)
-                    if j < last:
-                        times_gain(j - 1, d, everything)
+                    times_gain(j - 1, d, scalar_cols.get(j - 1, everything))
                 multiply(j, 1)
-                inverse_rms(j - 1, mean_square(j - 1, 0, DIMS), eps)
+                if j < last:
+                    inverse_rms(j - 1, mean_square(j - 1, 0, DIMS), eps)
+
+        def mean_square_on_vector(i, d):
+            squares = work.tile([P, C], F32, name="squares_v", tag="squares_v")
+            share = work.tile([P, 1], F32, name="share_v", tag="share_v")
+            nc.vector.scalar_tensor_tensor(
+                out=squares[:], in0=y[i][:, d, :], scalar=1.0 / (DIMS * C), in1=y[i][:, d, :],
+                op0=MULT, op1=MULT, accum_out=share[:],
+            )
+            return share
+
+        def inverse_rms_in_parts(i, part, other):
+            mean_sq[i] = work.tile([P, 1], F32, name="mean_sq", tag="mean_sq")
+            nc.scalar.activation(out=mean_sq[i][:], in_=part[:], func=ACT.Copy, bias=EPS)
+            inverse_rms(i, other, mean_sq[i])
 
         for d in range(DIMS):
             residual(last, d)
-            times_gain(last, d, halves[0])
-        share = mean_square(last, 0, 2)
-        mean_sq[last] = work.tile([P, 1], F32, name="mean_sq", tag="mean_sq")
-        nc.scalar.activation(out=mean_sq[last][:], in_=share[:], func=ACT.Copy, bias=EPS)
-        inverse_rms(last, mean_square(last, 2, DIMS), mean_sq[last])
-        for cols in halves:
-            normalise_on_vector(last - 1, cols)
-        normalise_on_scalar(last, halves[0])
-        normalise_on_vector(last, halves[1])
+            times_gain(last, d, scalar_cols[last])
+        part = mean_square(last - 1, 0, 2)
+        inverse_rms_in_parts(last - 1, part, mean_square(last - 1, 2, DIMS))
+        share_v = mean_square_on_vector(last, 2)
+        inverse_rms_in_parts(last, share_v, mean_square(last, 0, 2))
+        for i in (last - 1, last):
+            normalise_on_vector(i, vector_cols[i])
+            normalise_on_scalar(i, scalar_cols[i])

@@ -72,8 +72,6 @@ def tile_selfinteraction_pb_kernel(tc, s, v, g_v, wv, ln_g1, out):
         for i in range(2, TILES):
             load_rest(i)
 
-        warm = const.tile([P, C], BF16)
-        nc.vector.memset(warm[:], 0.0)
         ident_bf16 = const.tile([P, P], BF16)
         make_identity(nc, ident_bf16[:])
         ident_f32 = const.tile([P, P], F32)
@@ -105,14 +103,12 @@ def tile_selfinteraction_pb_kernel(tc, s, v, g_v, wv, ln_g1, out):
         u, u_codes, u_scales = {}, {}, {}
         acc, y, y_gain, mean_sq, inv_rms = {}, {}, {}, {}, {}
 
-        def warm_up(i, matmuls):
-            spare = psum_t.tile([P, C], F32, name="warm_ps", tag="sgT_ps")
-            for k in range(matmuls):
-                nc.tensor.matmul(spare[:], lhsT=warm[:, 0:P], rhs=warm[:], start=True, stop=True)
-
         def second_gate(i, engine):
-            sg_nat[i] = resident.tile([P, P, PACK], F32, name="sg_nat%d" % i)
-            engine.tensor_tensor(out=sg_nat[i][:], in0=s_sb[i][:], in1=g_sb[i][:, 1], op=MULT)
+            sg_nat[i] = resident.tile([P, PACK, P], F32, name="sg_nat%d" % i)
+            engine.tensor_tensor(
+                out=sg_nat[i][:], in0=s_sb[i][:].rearrange("n m t -> n t m"),
+                in1=g_sb[i][:, 1].rearrange("n m t -> n t m"), op=MULT,
+            )
 
         def transpose_first_gate(i):
             g1T_ps[i] = psum_t.tile([P, PACK // 2, P], F32, name="g1T_ps", tag="g1T_ps")
@@ -123,7 +119,7 @@ def tile_selfinteraction_pb_kernel(tc, s, v, g_v, wv, ln_g1, out):
         def transpose_second_gate(i):
             sgT_ps[i] = psum_t.tile([P, PACK, P], F32, name="sgT_ps", tag="sgT_ps")
             for t in range(PACK):
-                nc.tensor.transpose(sgT_ps[i][:, t, :], sg_nat[i][:, :, t], ident_f32[:])
+                nc.tensor.transpose(sgT_ps[i][:, t, :], sg_nat[i][:, t, :], ident_f32[:])
 
         def copy_first_gate(i):
             g1T[i] = work.tile([P, P, PACK], BF16, name="g1T", tag="g1T")
@@ -233,7 +229,6 @@ def tile_selfinteraction_pb_kernel(tc, s, v, g_v, wv, ln_g1, out):
         scalar_cols = {last - 1: slice(0, C // 2), last: slice(0, C // 4)}
         vector_cols = {i: slice(cols.stop, C) for i, cols in scalar_cols.items()}
 
-        warm_up(0, 4)
         second_gate(0, nc.vector)
         transpose_first_gate(0)
         copy_first_gate(0)
@@ -250,8 +245,6 @@ def tile_selfinteraction_pb_kernel(tc, s, v, g_v, wv, ln_g1, out):
                 transpose_second_gate(j + 1)
                 copy_first_gate(j + 1)
                 copy_second_gate(j + 1)
-            if j == last:
-                warm_up(j, 4)
             if j == 0:
                 for h in range(PASSES):
                     group_wv(h)

@@ -33,7 +33,7 @@ def tile_selfinteraction_pb_kernel(tc, s, v, g_v, wv, ln_g1, out):
         resident = ctx.enter_context(tc.tile_pool(name="resident", bufs=1))
         work = ctx.enter_context(tc.tile_pool(name="work", bufs=2))
         psum_t = ctx.enter_context(tc.psum_pool(name="psum_t", bufs=1))
-        psum_acc = ctx.enter_context(tc.psum_pool(name="psum_acc", bufs=4))
+        psum_acc = ctx.enter_context(tc.psum_pool(name="psum_acc", bufs=3))
         ctx.enter_context(tc.manual_schedule())
 
         g_sb = [resident.tile([P, PASSES, P, PACK], BF16, name="g_sb%d" % i) for i in range(TILES)]
@@ -74,6 +74,9 @@ def tile_selfinteraction_pb_kernel(tc, s, v, g_v, wv, ln_g1, out):
 
         ident_bf16 = const.tile([P, P], BF16)
         make_identity(nc, ident_bf16[:])
+        ident_wide = const.tile([P, P + 4], BF16)
+        nc.vector.memset(ident_wide[:], 0.0)
+        make_identity(nc, ident_wide[:, 2 : P + 2])
         ident_f32 = const.tile([P, P], F32)
         make_identity(nc, ident_f32[:])
         one = const.tile([P, 1], F32)
@@ -99,7 +102,7 @@ def tile_selfinteraction_pb_kernel(tc, s, v, g_v, wv, ln_g1, out):
             )
 
         last = TILES - 1
-        sg_nat, g1T_ps, sgT_ps, g1T, sgT, vT_ps = {}, {}, {}, {}, {}, {}
+        sg_nat, g1T_ps, sgT_ps, g1T, sgT, vT = {}, {}, {}, {}, {}, {}
         u, u_codes, u_scales = {}, {}, {}
         acc, y, y_gain, mean_sq, inv_rms = {}, {}, {}, {}, {}
 
@@ -130,22 +133,29 @@ def tile_selfinteraction_pb_kernel(tc, s, v, g_v, wv, ln_g1, out):
             nc.scalar.mul(out=sgT[i][:], in_=sgT_ps[i][:].rearrange("p t n -> p n t"), mul=math.sqrt(2.0))
 
         def transpose_v(i, k):
-            vT_ps[i, k] = psum_t.tile([P, len(GROUPS[k]), PACK, P], BF16, name="vT_ps%d" % k, tag="vT_ps%d" % k)
-            for e, d in enumerate(GROUPS[k]):
-                for t in range(PACK):
-                    nc.tensor.transpose(vT_ps[i, k][:, e, t, :], v_sb[i][:, t:C:PACK, d], ident_bf16[:])
+            for d in GROUPS[k]:
+                if k == 0:
+                    bank = psum_t.tile([P, PACK, P], BF16, name="vT_ps0", tag="vT_ps0")
+                    for t in range(PACK):
+                        nc.tensor.transpose(bank[:, t, :], v_sb[i][:, t:C:PACK, d], ident_bf16[:])
+                    vT[i, d] = bank[:].rearrange("p t n -> p n t")
+                else:
+                    bank = psum_t.tile([P, P + 2, PACK + 1], BF16, name="vT_ps%d" % d, tag="vT_ps%d" % d)
+                    for t in range(PACK):
+                        first = 1 if t % 2 else 0
+                        nc.tensor.matmul(
+                            bank[:, first : P + 1 + first, t], lhsT=v_sb[i][:, t:C:PACK, d],
+                            rhs=ident_wide[:, 1 + first : P + 2 + first], start=True, stop=True,
+                        )
+                    vT[i, d] = bank[:, 1 : P + 1, 0:PACK]
 
         def product(i, k, h, gate):
             if h == 0:
                 u[i, k] = work.tile(
                     [P, PASSES, len(GROUPS[k]), P, PACK], BF16, name="u%d" % k, tag="u%d" % k, align_bytes=64
                 )
-            nc.vector.tensor_tensor(
-                out=u[i, k][:, h],
-                in0=vT_ps[i, k][:].rearrange("p e t n -> p e n t"),
-                in1=gate[:].unsqueeze(1).to_broadcast([P, len(GROUPS[k]), P, PACK]),
-                op=MULT,
-            )
+            for e, d in enumerate(GROUPS[k]):
+                nc.vector.tensor_tensor(out=u[i, k][:, h, e], in0=vT[i, d], in1=gate[:], op=MULT)
 
         def quantise(i, k):
             shape = [P, PASSES, len(GROUPS[k]), P]
@@ -159,8 +169,8 @@ def tile_selfinteraction_pb_kernel(tc, s, v, g_v, wv, ln_g1, out):
 
         def multiply(i, k):
             for e, d in enumerate(GROUPS[k]):
-                if i == last and d > 0:
-                    acc[i, d] = psum_t.tile([P, C], F32, name="acc", tag="vT_ps%d" % (d - 1))
+                if i == last:
+                    acc[i, d] = psum_t.tile([P, C], F32, name="acc", tag="vT_ps%d" % d)
                 else:
                     acc[i, d] = psum_acc.tile([P, C], F32, name="acc", tag="acc")
                 for h in range(PASSES):
@@ -225,8 +235,8 @@ def tile_selfinteraction_pb_kernel(tc, s, v, g_v, wv, ln_g1, out):
             )
             store(i, cols, result)
 
-        everything = slice(0, C)
-        scalar_cols = {last - 1: slice(0, C // 2), last: slice(0, C // 4)}
+        scalar_cols = {i: slice(0, 3 * C // 4) for i in range(last - 1)}
+        scalar_cols[last - 1], scalar_cols[last] = slice(0, C // 2), slice(0, C // 4)
         vector_cols = {i: slice(cols.stop, C) for i, cols in scalar_cols.items()}
 
         second_gate(0, nc.vector)
@@ -249,7 +259,7 @@ def tile_selfinteraction_pb_kernel(tc, s, v, g_v, wv, ln_g1, out):
                 for h in range(PASSES):
                     group_wv(h)
             if j >= 2:
-                normalise_on_scalar(j - 2, everything)
+                normalise_on_scalar(j - 2, scalar_cols[j - 2])
             product(j, 0, 0, g1T[j])
             product(j, 1, 0, g1T[j])
             product(j, 0, 1, sgT[j])
@@ -268,11 +278,13 @@ def tile_selfinteraction_pb_kernel(tc, s, v, g_v, wv, ln_g1, out):
             if j >= 1:
                 quantise(j, 0)
                 quantise(j, 1)
+            if j >= 2:
+                normalise_on_vector(j - 2, vector_cols[j - 2])
             if j >= 1:
                 multiply(j, 0)
                 for d in range(DIMS):
                     residual(j - 1, d)
-                    times_gain(j - 1, d, scalar_cols.get(j - 1, everything))
+                    times_gain(j - 1, d, scalar_cols[j - 1])
                 multiply(j, 1)
                 if j < last:
                     inverse_rms(j - 1, mean_square(j - 1, 0, DIMS), eps)

@@ -192,11 +192,13 @@ def tile_selfinteraction_pb_kernel(tc, s, v, g_v, wv, ln_g1, out):
                 in1=v_sb[i][:, :, d], op0=MULT, op1=ADD,
             )
 
-        def times_gain(i, d, cols):
-            if d == 0:
+        def times_gain(i, first, stop):
+            if first == 0:
                 y_gain[i] = work.tile([P, DIMS, C], F32, name="y_gain", tag="y_gain")
+            cols = scalar_cols[i]
             nc.gpsimd.tensor_tensor(
-                out=y_gain[i][:, d, cols], in0=y[i][:, d, cols], in1=gain[:, cols], op=MULT
+                out=y_gain[i][:, first:stop, cols], in0=y[i][:, first:stop, cols],
+                in1=gain[:, cols].unsqueeze(1).to_broadcast([P, stop - first, cols.stop]), op=MULT,
             )
 
         def mean_square(i, first, last):
@@ -235,17 +237,17 @@ def tile_selfinteraction_pb_kernel(tc, s, v, g_v, wv, ln_g1, out):
             )
             store(i, cols, result)
 
-        scalar_cols = {i: slice(0, 3 * C // 4) for i in range(last - 1)}
+        scalar_cols = {i: slice(0, 7 * C // 8) for i in range(last - 1)}
         scalar_cols[last - 1], scalar_cols[last] = slice(0, C // 2), slice(0, C // 4)
         vector_cols = {i: slice(cols.stop, C) for i, cols in scalar_cols.items()}
 
         second_gate(0, nc.vector)
         transpose_first_gate(0)
         copy_first_gate(0)
-        transpose_v(0, 0)
-        transpose_v(0, 1)
         transpose_second_gate(0)
         copy_second_gate(0)
+        transpose_v(0, 0)
+        transpose_v(0, 1)
         for i in range(1, TILES):
             second_gate(i, nc.gpsimd)
 
@@ -261,10 +263,10 @@ def tile_selfinteraction_pb_kernel(tc, s, v, g_v, wv, ln_g1, out):
             if j >= 2:
                 normalise_on_scalar(j - 2, scalar_cols[j - 2])
             product(j, 0, 0, g1T[j])
-            product(j, 1, 0, g1T[j])
             product(j, 0, 1, sgT[j])
             if j < last:
                 transpose_v(j + 1, 0)
+            product(j, 1, 0, g1T[j])
             product(j, 1, 1, sgT[j])
             if j < last:
                 transpose_v(j + 1, 1)
@@ -284,10 +286,16 @@ def tile_selfinteraction_pb_kernel(tc, s, v, g_v, wv, ln_g1, out):
                 multiply(j, 0)
                 for d in range(DIMS):
                     residual(j - 1, d)
-                    times_gain(j - 1, d, scalar_cols[j - 1])
+                    if d != 1:
+                        times_gain(j - 1, max(d - 1, 0), d + 1)
                 multiply(j, 1)
                 if j < last:
                     inverse_rms(j - 1, mean_square(j - 1, 0, DIMS), eps)
+
+        def inverse_rms_in_parts(i, part, other):
+            mean_sq[i] = work.tile([P, 1], F32, name="mean_sq", tag="mean_sq")
+            nc.scalar.activation(out=mean_sq[i][:], in_=part[:], func=ACT.Copy, bias=EPS)
+            inverse_rms(i, other, mean_sq[i])
 
         def mean_square_on_vector(i, d):
             squares = work.tile([P, C], F32, name="squares_v", tag="squares_v")
@@ -298,14 +306,10 @@ def tile_selfinteraction_pb_kernel(tc, s, v, g_v, wv, ln_g1, out):
             )
             return share
 
-        def inverse_rms_in_parts(i, part, other):
-            mean_sq[i] = work.tile([P, 1], F32, name="mean_sq", tag="mean_sq")
-            nc.scalar.activation(out=mean_sq[i][:], in_=part[:], func=ACT.Copy, bias=EPS)
-            inverse_rms(i, other, mean_sq[i])
-
         for d in range(DIMS):
             residual(last, d)
-            times_gain(last, d, scalar_cols[last])
+            if d != 1:
+                times_gain(last, max(d - 1, 0), d + 1)
         part = mean_square(last - 1, 0, 2)
         inverse_rms_in_parts(last - 1, part, mean_square(last - 1, 2, DIMS))
         share_v = mean_square_on_vector(last, 2)

@@ -63,17 +63,16 @@ def tile_selfinteraction_pb_kernel(tc, s, v, g_v, wv, ln_g1, out):
             )
         load_second_gate(0)
         load_rest(0)
-        for i in range(1, TILES):
-            load_second_gate(i)
+        load_second_gate(1)
         load_rest(1)
+        for i in range(2, TILES):
+            load_second_gate(i)
         for h in range(PASSES):
             load_wv(h)
         nc.sync.dma_start(out=gain[:], in_=ln_g1.partition_broadcast(P))
         for i in range(2, TILES):
             load_rest(i)
 
-        ident_bf16 = const.tile([P, P], BF16)
-        make_identity(nc, ident_bf16[:])
         ident_wide = const.tile([P, P + 4], BF16)
         nc.vector.memset(ident_wide[:], 0.0)
         make_identity(nc, ident_wide[:, 2 : P + 2])
@@ -89,10 +88,10 @@ def tile_selfinteraction_pb_kernel(tc, s, v, g_v, wv, ln_g1, out):
         wv_codes = const.tile([P, PASSES, C], U32, align_bytes=64)
         wv_scales = const.tile([P, PASSES, C], U8, align_bytes=64)
 
-        def group_wv(h):
-            dst = wv_grouped[:, h].rearrange("p (c i) t -> p c t i", i=4)
-            src = wv_sb[h][:].rearrange("p t (c i) -> p c t i", i=4)
-            nc.scalar.copy(out=dst, in_=src)
+        def group_wv(copy, h, cols):
+            dst = wv_grouped[:, h, cols].rearrange("p (c i) t -> p c t i", i=4)
+            src = wv_sb[h][:, :, cols].rearrange("p t (c i) -> p c t i", i=4)
+            copy(out=dst, in_=src)
 
         def quantise_wv(h):
             nc.vector.quantize_mx(
@@ -103,6 +102,7 @@ def tile_selfinteraction_pb_kernel(tc, s, v, g_v, wv, ln_g1, out):
 
         last = TILES - 1
         sg_nat, g1T_ps, sgT_ps, g1T, sgT, vT = {}, {}, {}, {}, {}, {}
+        v_words = {}
         u, u_codes, u_scales = {}, {}, {}
         acc, y, y_gain, mean_sq, inv_rms = {}, {}, {}, {}, {}
 
@@ -132,30 +132,37 @@ def tile_selfinteraction_pb_kernel(tc, s, v, g_v, wv, ln_g1, out):
             sgT[i] = work.tile([P, P, PACK], F32, name="sgT", tag="sgT")
             nc.scalar.mul(out=sgT[i][:], in_=sgT_ps[i][:].rearrange("p t n -> p n t"), mul=math.sqrt(2.0))
 
-        def transpose_v(i, k):
-            for d in GROUPS[k]:
-                if k == 0:
-                    bank = psum_t.tile([P, PACK, P], BF16, name="vT_ps0", tag="vT_ps0")
-                    for t in range(PACK):
-                        nc.tensor.transpose(bank[:, t, :], v_sb[i][:, t:C:PACK, d], ident_bf16[:])
-                    vT[i, d] = bank[:].rearrange("p t n -> p n t")
-                else:
-                    bank = psum_t.tile([P, P + 2, PACK + 1], BF16, name="vT_ps%d" % d, tag="vT_ps%d" % d)
-                    for t in range(PACK):
-                        first = 1 if t % 2 else 0
-                        nc.tensor.matmul(
-                            bank[:, first : P + 1 + first, t], lhsT=v_sb[i][:, t:C:PACK, d],
-                            rhs=ident_wide[:, 1 + first : P + 2 + first], start=True, stop=True,
-                        )
-                    vT[i, d] = bank[:, 1 : P + 1, 0:PACK]
+        def gather_words(i):
+            v_words[i] = work.tile([P, PACK // 2, P, 2], BF16, name="v_words", tag="v_words")
+            nc.scalar.copy(
+                out=v_words[i][:], in_=v_sb[i][:, :, DIMS - 1].rearrange("n (p w q) -> n w p q", w=PACK // 2, q=2)
+            )
 
-        def product(i, k, h, gate):
-            if h == 0:
+        def turn_v(i, d):
+            if d < DIMS - 1:
+                bank = psum_t.tile([P, P + 2, PACK + 1], BF16, name="vT_ps%d" % d, tag="vT_ps%d" % d)
+                for t in range(PACK):
+                    first = 1 if t % 2 else 0
+                    nc.tensor.matmul(
+                        bank[:, first : P + 1 + first, t], lhsT=v_sb[i][:, t:C:PACK, d],
+                        rhs=ident_wide[:, 1 + first : P + 2 + first], start=True, stop=True,
+                    )
+                vT[i, d] = bank[:, 1 : P + 1, 0:PACK]
+            else:
+                bank = psum_t.tile([P, P, PACK], BF16, name="vT_ps%d" % d, tag="vT_ps%d" % d)
+                words = v_words[i][:].rearrange("n w p q -> n w (p q)").bitcast(F32)
+                for w in range(PACK // 2):
+                    nc.tensor.transpose(bank[:].bitcast(F32)[:, :, w], words[:, w, :], ident_f32[:])
+                vT[i, d] = bank[:]
+
+        def product(i, d, h, gate):
+            k = 0 if d in GROUPS[0] else 1
+            e = GROUPS[k].index(d)
+            if h == 0 and e == 0:
                 u[i, k] = work.tile(
                     [P, PASSES, len(GROUPS[k]), P, PACK], BF16, name="u%d" % k, tag="u%d" % k, align_bytes=64
                 )
-            for e, d in enumerate(GROUPS[k]):
-                nc.vector.tensor_tensor(out=u[i, k][:, h, e], in0=vT[i, d], in1=gate[:], op=MULT)
+            nc.vector.tensor_tensor(out=u[i, k][:, h, e], in0=vT[i, d], in1=gate[:], op=MULT)
 
         def quantise(i, k):
             shape = [P, PASSES, len(GROUPS[k]), P]
@@ -218,7 +225,7 @@ def tile_selfinteraction_pb_kernel(tc, s, v, g_v, wv, ln_g1, out):
             nc.sync.dma_start(out=out[i * P : (i + 1) * P, cols, :], in_=result)
 
         def new_result(cols):
-            tile = work.tile([P, C, DIMS], F32, name="result", tag="result", bufs=4)
+            tile = work.tile([P, C, DIMS], F32, name="result", tag="result", bufs=7)
             return tile[:, 0 : cols.stop - cols.start, :]
 
         def normalise_on_scalar(i, cols):
@@ -239,15 +246,18 @@ def tile_selfinteraction_pb_kernel(tc, s, v, g_v, wv, ln_g1, out):
 
         scalar_cols = {i: slice(0, 7 * C // 8) for i in range(last - 1)}
         scalar_cols[last - 1], scalar_cols[last] = slice(0, C // 2), slice(0, C // 4)
-        vector_cols = {i: slice(cols.stop, C) for i, cols in scalar_cols.items()}
+        vector_cols = {i: [slice(cols.stop, C)] for i, cols in scalar_cols.items()}
+        middle = (scalar_cols[last].stop + C) // 2
+        vector_cols[last] = [slice(scalar_cols[last].stop, middle), slice(middle, C)]
 
         second_gate(0, nc.vector)
         transpose_first_gate(0)
         copy_first_gate(0)
         transpose_second_gate(0)
         copy_second_gate(0)
-        transpose_v(0, 0)
-        transpose_v(0, 1)
+        gather_words(0)
+        for d in range(DIMS):
+            turn_v(0, d)
         for i in range(1, TILES):
             second_gate(i, nc.gpsimd)
 
@@ -255,24 +265,23 @@ def tile_selfinteraction_pb_kernel(tc, s, v, g_v, wv, ln_g1, out):
             if j < last:
                 transpose_first_gate(j + 1)
                 transpose_second_gate(j + 1)
+                gather_words(j + 1)
                 copy_first_gate(j + 1)
                 copy_second_gate(j + 1)
             if j == 0:
-                for h in range(PASSES):
-                    group_wv(h)
+                group_wv(nc.scalar.copy, 0, slice(0, C))
+                group_wv(nc.scalar.copy, 1, slice(0, C // 2))
             if j >= 2:
                 normalise_on_scalar(j - 2, scalar_cols[j - 2])
-            product(j, 0, 0, g1T[j])
-            product(j, 0, 1, sgT[j])
-            if j < last:
-                transpose_v(j + 1, 0)
-            product(j, 1, 0, g1T[j])
-            product(j, 1, 1, sgT[j])
-            if j < last:
-                transpose_v(j + 1, 1)
+            for d in range(DIMS):
+                product(j, d, 0, g1T[j])
+                product(j, d, 1, sgT[j])
+                if j < last:
+                    turn_v(j + 1, d)
             if j == 1:
                 quantise(0, 0)
                 quantise(0, 1)
+                group_wv(nc.vector.tensor_copy, 1, slice(C // 2, C))
                 for h in range(PASSES):
                     quantise_wv(h)
                 multiply(0, 0)
@@ -281,7 +290,8 @@ def tile_selfinteraction_pb_kernel(tc, s, v, g_v, wv, ln_g1, out):
                 quantise(j, 0)
                 quantise(j, 1)
             if j >= 2:
-                normalise_on_vector(j - 2, vector_cols[j - 2])
+                for cols in vector_cols[j - 2]:
+                    normalise_on_vector(j - 2, cols)
             if j >= 1:
                 multiply(j, 0)
                 for d in range(DIMS):
@@ -315,5 +325,6 @@ def tile_selfinteraction_pb_kernel(tc, s, v, g_v, wv, ln_g1, out):
         share_v = mean_square_on_vector(last, 2)
         inverse_rms_in_parts(last, share_v, mean_square(last, 0, 2))
         for i in (last - 1, last):
-            normalise_on_vector(i, vector_cols[i])
+            normalise_on_vector(i, vector_cols[i][0])
             normalise_on_scalar(i, scalar_cols[i])
+        normalise_on_vector(last, vector_cols[last][1])

@@ -40,6 +40,8 @@ def tile_selfinteraction_pb_kernel(tc, s, v, g_v, wv, ln_g1, out):
         s_sb = [resident.tile([P, P, PACK], BF16, name="s_sb%d" % i) for i in range(TILES)]
         v_sb = [resident.tile([P, C, DIMS], BF16, name="v_sb%d" % i) for i in range(TILES)]
         wv_sb = [resident.tile([P, PACK, C], BF16, name="wv_sb%d" % h) for h in range(PASSES)]
+        gain_row = const.tile([P, C], BF16)
+        nc.vector.memset(gain_row[:], 0.0)
         gain = const.tile([P, C], BF16)
 
         def load_gate(i, h):
@@ -65,14 +67,16 @@ def tile_selfinteraction_pb_kernel(tc, s, v, g_v, wv, ln_g1, out):
         load_rest(0)
         load_second_gate(1)
         load_rest(1)
+        nc.sync.dma_start(out=gain_row[0:1, :], in_=ln_g1.unsqueeze(0))
         for i in range(2, TILES):
             load_second_gate(i)
         for h in range(PASSES):
             load_wv(h)
-        nc.sync.dma_start(out=gain[:], in_=ln_g1.partition_broadcast(P))
         for i in range(2, TILES):
             load_rest(i)
 
+        ones = const.tile([P, P], BF16)
+        nc.vector.memset(ones[:], 1.0)
         ident_wide = const.tile([P, P + 4], BF16)
         nc.vector.memset(ident_wide[:], 0.0)
         make_identity(nc, ident_wide[:, 2 : P + 2])
@@ -105,6 +109,11 @@ def tile_selfinteraction_pb_kernel(tc, s, v, g_v, wv, ln_g1, out):
         v_words = {}
         u, u_codes, u_scales = {}, {}, {}
         acc, y, y_gain, mean_sq, inv_rms = {}, {}, {}, {}, {}
+
+        def spread_gain():
+            spread = psum_acc.tile([P, C], F32, name="spread", tag="acc")
+            nc.tensor.matmul(spread[:], lhsT=ones[:], rhs=gain_row[:], start=True, stop=True)
+            nc.scalar.copy(out=gain[:], in_=spread[:])
 
         def second_gate(i, engine):
             sg_nat[i] = resident.tile([P, PACK, P], F32, name="sg_nat%d" % i)
@@ -271,6 +280,8 @@ def tile_selfinteraction_pb_kernel(tc, s, v, g_v, wv, ln_g1, out):
             if j == 0:
                 group_wv(nc.scalar.copy, 0, slice(0, C))
                 group_wv(nc.scalar.copy, 1, slice(0, C // 2))
+            if j == 1:
+                spread_gain()
             if j >= 2:
                 normalise_on_scalar(j - 2, scalar_cols[j - 2])
             for d in range(DIMS):

@@ -65,10 +65,11 @@ def tile_selfinteraction_pb_kernel(tc, s, v, g_v, wv, ln_g1, out):
             )
         load_second_gate(0)
         load_rest(0)
-        load_second_gate(1)
+        for i in (1, 2):
+            load_second_gate(i)
         load_rest(1)
         nc.sync.dma_start(out=gain_row[0:1, :], in_=ln_g1.unsqueeze(0))
-        for i in range(2, TILES):
+        for i in range(3, TILES):
             load_second_gate(i)
         for h in range(PASSES):
             load_wv(h)
@@ -108,19 +109,22 @@ def tile_selfinteraction_pb_kernel(tc, s, v, g_v, wv, ln_g1, out):
         sg_nat, g1T_ps, sgT_ps, g1T, sgT, vT = {}, {}, {}, {}, {}, {}
         v_words = {}
         u, u_codes, u_scales = {}, {}, {}
-        acc, y, y_gain, mean_sq, inv_rms = {}, {}, {}, {}, {}
+        acc, y, y_gain, inv_rms = {}, {}, {}, {}
 
         def spread_gain():
             spread = psum_acc.tile([P, C], F32, name="spread", tag="acc")
             nc.tensor.matmul(spread[:], lhsT=ones[:], rhs=gain_row[:], start=True, stop=True)
             nc.scalar.copy(out=gain[:], in_=spread[:])
 
-        def second_gate(i, engine):
+        def second_gate(i, engine, pieces=1):
             sg_nat[i] = resident.tile([P, PACK, P], F32, name="sg_nat%d" % i)
-            engine.tensor_tensor(
-                out=sg_nat[i][:], in0=s_sb[i][:].rearrange("n m t -> n t m"),
-                in1=g_sb[i][:, 1].rearrange("n m t -> n t m"), op=MULT,
-            )
+            width = PACK // pieces
+            for first in range(0, PACK, width):
+                ts = slice(first, first + width)
+                engine.tensor_tensor(
+                    out=sg_nat[i][:, ts], in0=s_sb[i][:, :, ts].rearrange("n m t -> n t m"),
+                    in1=g_sb[i][:, 1, :, ts].rearrange("n m t -> n t m"), op=MULT,
+                )
 
         def transpose_first_gate(i):
             g1T_ps[i] = psum_t.tile([P, PACK // 2, P], F32, name="g1T_ps", tag="g1T_ps")
@@ -259,7 +263,7 @@ def tile_selfinteraction_pb_kernel(tc, s, v, g_v, wv, ln_g1, out):
         middle = (scalar_cols[last].stop + C) // 2
         vector_cols[last] = [slice(scalar_cols[last].stop, middle), slice(middle, C)]
 
-        second_gate(0, nc.vector)
+        second_gate(0, nc.vector, pieces=2)
         transpose_first_gate(0)
         copy_first_gate(0)
         transpose_second_gate(0)
@@ -274,9 +278,12 @@ def tile_selfinteraction_pb_kernel(tc, s, v, g_v, wv, ln_g1, out):
             if j < last:
                 transpose_first_gate(j + 1)
                 transpose_second_gate(j + 1)
-                gather_words(j + 1)
+                if j > 0:
+                    gather_words(j + 1)
                 copy_first_gate(j + 1)
                 copy_second_gate(j + 1)
+                if j == 0:
+                    gather_words(j + 1)
             if j == 0:
                 group_wv(nc.scalar.copy, 0, slice(0, C))
                 group_wv(nc.scalar.copy, 1, slice(0, C // 2))
@@ -313,10 +320,11 @@ def tile_selfinteraction_pb_kernel(tc, s, v, g_v, wv, ln_g1, out):
                 if j < last:
                     inverse_rms(j - 1, mean_square(j - 1, 0, DIMS), eps)
 
-        def inverse_rms_in_parts(i, part, other):
-            mean_sq[i] = work.tile([P, 1], F32, name="mean_sq", tag="mean_sq")
-            nc.scalar.activation(out=mean_sq[i][:], in_=part[:], func=ACT.Copy, bias=EPS)
-            inverse_rms(i, other, mean_sq[i])
+        def add_shares(first, second):
+            sums = [work.tile([P, 1], F32, name="mean_sq", tag="mean_sq", bufs=4) for k in range(2)]
+            nc.scalar.activation(out=sums[0][:], in_=first[:], func=ACT.Copy, bias=EPS)
+            nc.scalar.activation(out=sums[1][:], in_=second[:], func=ACT.Identity, bias=sums[0][:])
+            return sums[1]
 
         def mean_square_on_vector(i, d):
             squares = work.tile([P, C], F32, name="squares_v", tag="squares_v")
@@ -331,10 +339,10 @@ def tile_selfinteraction_pb_kernel(tc, s, v, g_v, wv, ln_g1, out):
             residual(last, d)
             if d != 1:
                 times_gain(last, max(d - 1, 0), d + 1)
-        part = mean_square(last - 1, 0, 2)
-        inverse_rms_in_parts(last - 1, part, mean_square(last - 1, 2, DIMS))
-        share_v = mean_square_on_vector(last, 2)
-        inverse_rms_in_parts(last, share_v, mean_square(last, 0, 2))
+        for i in (last - 1, last):
+            two = add_shares(mean_square(i, 0, 1), mean_square(i, 1, 2))
+            third = mean_square_on_vector(i, 2) if i == last else mean_square(i, 2, DIMS)
+            inverse_rms(i, third, two)
         for i in (last - 1, last):
             normalise_on_vector(i, vector_cols[i][0])
             normalise_on_scalar(i, scalar_cols[i])

from contextlib import ExitStack
import math

import concourse.mybir as mybir
from concourse.masks import make_identity

BF16 = mybir.dt.bfloat16
F32 = mybir.dt.float32
U32 = mybir.dt.uint32
U8 = mybir.dt.uint8
FP8X4 = mybir.dt.float8_e4m3fn_x4
MULT = mybir.AluOpType.mult
ADD = mybir.AluOpType.add
ACT = mybir.ActivationFunctionType

P = 128
PACK = 4
POINTS = 768
C = 512
DIMS = 3
PASSES = 2
TILES = POINTS // P
EPS = 1e-6
GROUPS = ((0,), (1, 2))

FLOPS = 2 * POINTS * DIMS * (PASSES * C) * C


def tile_selfinteraction_pb_kernel(tc, s, v, g_v, wv, ln_g1, out):
    nc = tc.nc
    with ExitStack() as ctx:
        const = ctx.enter_context(tc.tile_pool(name="const", bufs=1))
        resident = ctx.enter_context(tc.tile_pool(name="resident", bufs=1))
        work = ctx.enter_context(tc.tile_pool(name="work", bufs=2))
        psum_t = ctx.enter_context(tc.psum_pool(name="psum_t", bufs=1))
        psum_acc = ctx.enter_context(tc.psum_pool(name="psum_acc", bufs=3))
        ctx.enter_context(tc.manual_schedule())

        g_sb = [resident.tile([P, PASSES, P, PACK], BF16, name="g_sb%d" % i) for i in range(TILES)]
        s_sb = [resident.tile([P, P, PACK], BF16, name="s_sb%d" % i) for i in range(TILES)]
        v_sb = [resident.tile([P, C, DIMS], BF16, name="v_sb%d" % i) for i in range(TILES)]
        wv_sb = [resident.tile([P, PACK, C], BF16, name="wv_sb%d" % h) for h in range(PASSES)]
        gain_row = const.tile([P, C], BF16)
        nc.vector.memset(gain_row[:], 0.0)
        gain = const.tile([P, C], BF16)

        def load_gate(i, h):
            rows = slice(i * P, (i + 1) * P)
            nc.sync.dma_start(
                out=g_sb[i][:, h], in_=g_v[rows, h * C : (h + 1) * C].rearrange("n (m t) -> n m t", t=PACK)
            )

        def load_second_gate(i):
            load_gate(i, 1)
            nc.sync.dma_start(out=s_sb[i][:], in_=s[i * P : (i + 1) * P, :].rearrange("n (m t) -> n m t", t=PACK))

        def load_rest(i):
            load_gate(i, 0)
            nc.sync.dma_start(out=v_sb[i][:], in_=v[i * P : (i + 1) * P, :, :])

        def load_wv(h):
            nc.sync.dma_start(
                out=wv_sb[h][:],
                in_=wv[h * PACK * P : (h + 1) * PACK * P, :].rearrange("(p t) c -> p t c", t=PACK),
            )
        load_second_gate(0)
        load_rest(0)
        for i in (1, 2):
            load_second_gate(i)
        load_rest(1)
        nc.sync.dma_start(out=gain_row[0:1, :], in_=ln_g1.unsqueeze(0))
        for i in range(3, TILES):
            load_second_gate(i)
        for h in range(PASSES):
            load_wv(h)
        for i in range(2, TILES):
            load_rest(i)

        ones = const.tile([P, P], BF16)
        nc.vector.memset(ones[:], 1.0)
        ident_wide = const.tile([P, P + 4], BF16)
        nc.vector.memset(ident_wide[:], 0.0)
        make_identity(nc, ident_wide[:, 2 : P + 2])
        ident_f32 = const.tile([P, P], F32)
        make_identity(nc, ident_f32[:])
        one = const.tile([P, 1], F32)
        nc.vector.memset(one[:], 1.0)
        nc.scalar.activation(out=one[:], in_=one[:], func=ACT.Abs_reciprocal_sqrt)
        eps = const.tile([P, 1], F32)
        nc.scalar.activation(out=eps[:], in_=one[:], func=ACT.Copy, scale=0.0, bias=EPS)

        wv_grouped = const.tile([P, PASSES, C, PACK], BF16, align_bytes=64)
        wv_codes = const.tile([P, PASSES, C], U32, align_bytes=64)
        wv_scales = const.tile([P, PASSES, C], U8, align_bytes=64)

        def group_wv(copy, h, cols):
            dst = wv_grouped[:, h, cols].rearrange("p (c i) t -> p c t i", i=4)
            src = wv_sb[h][:, :, cols].rearrange("p t (c i) -> p c t i", i=4)
            copy(out=dst, in_=src)

        def quantise_wv(h):
            nc.vector.quantize_mx(
                out=wv_codes[:, h, :].bitcast(FP8X4),
                scales=wv_scales[:, h, :],
                in_=wv_grouped[:, h].rearrange("p c t -> p (c t)"),
            )

        last = TILES - 1
        sg_nat, g1T_ps, sgT_ps, g1T, sgT, vT = {}, {}, {}, {}, {}, {}
        v_words = {}
        u, u_codes, u_scales = {}, {}, {}
        acc, y, y_gain, inv_rms = {}, {}, {}, {}

        def spread_gain():
            spread = psum_acc.tile([P, C], F32, name="spread", tag="acc")
            nc.tensor.matmul(spread[:], lhsT=ones[:], rhs=gain_row[:], start=True, stop=True)
            nc.scalar.copy(out=gain[:], in_=spread[:])

        def second_gate(i, engine, pieces=1):
            sg_nat[i] = resident.tile([P, PACK, P], F32, name="sg_nat%d" % i)
            width = PACK // pieces
            for first in range(0, PACK, width):
                ts = slice(first, first + width)
                engine.tensor_tensor(
                    out=sg_nat[i][:, ts], in0=s_sb[i][:, :, ts].rearrange("n m t -> n t m"),
                    in1=g_sb[i][:, 1, :, ts].rearrange("n m t -> n t m"), op=MULT,
                )

        def transpose_first_gate(i):
            g1T_ps[i] = psum_t.tile([P, PACK // 2, P], F32, name="g1T_ps", tag="g1T_ps")
            words = g_sb[i][:, 0].bitcast(F32)
            for w in range(PACK // 2):
                nc.tensor.transpose(g1T_ps[i][:, w, :], words[:, :, w], ident_f32[:])

        def transpose_second_gate(i):
            sgT_ps[i] = psum_t.tile([P, PACK, P], F32, name="sgT_ps", tag="sgT_ps")
            for t in range(PACK):
                nc.tensor.transpose(sgT_ps[i][:, t, :], sg_nat[i][:, t, :], ident_f32[:])

        def copy_first_gate(i):
            g1T[i] = work.tile([P, P, PACK], BF16, name="g1T", tag="g1T")
            nc.scalar.copy(out=g1T[i][:].bitcast(F32), in_=g1T_ps[i][:].rearrange("p w n -> p n w"))

        def copy_second_gate(i):
            sgT[i] = work.tile([P, P, PACK], F32, name="sgT", tag="sgT")
            nc.scalar.mul(out=sgT[i][:], in_=sgT_ps[i][:].rearrange("p t n -> p n t"), mul=math.sqrt(2.0))

        def gather_words(i):
            v_words[i] = work.tile([P, PACK // 2, P, 2], BF16, name="v_words", tag="v_words")
            nc.scalar.copy(
                out=v_words[i][:], in_=v_sb[i][:, :, DIMS - 1].rearrange("n (p w q) -> n w p q", w=PACK // 2, q=2)
            )

        def turn_v(i, d):
            if d < DIMS - 1:
                bank = psum_t.tile([P, P + 2, PACK + 1], BF16, name="vT_ps%d" % d, tag="vT_ps%d" % d)
                for t in range(PACK):
                    first = 1 if t % 2 else 0
                    nc.tensor.matmul(
                        bank[:, first : P + 1 + first, t], lhsT=v_sb[i][:, t:C:PACK, d],
                        rhs=ident_wide[:, 1 + first : P + 2 + first], start=True, stop=True,
                    )
                vT[i, d] = bank[:, 1 : P + 1, 0:PACK]
            else:
                bank = psum_t.tile([P, P, PACK], BF16, name="vT_ps%d" % d, tag="vT_ps%d" % d)
                words = v_words[i][:].rearrange("n w p q -> n w (p q)").bitcast(F32)
                for w in range(PACK // 2):
                    nc.tensor.transpose(bank[:].bitcast(F32)[:, :, w], words[:, w, :], ident_f32[:])
                vT[i, d] = bank[:]

        def product(i, d, h, gate):
            k = 0 if d in GROUPS[0] else 1
            e = GROUPS[k].index(d)
            if h == 0 and e == 0:
                u[i, k] = work.tile(
                    [P, PASSES, len(GROUPS[k]), P, PACK], BF16, name="u%d" % k, tag="u%d" % k, align_bytes=64
                )
            nc.vector.tensor_tensor(out=u[i, k][:, h, e], in0=vT[i, d], in1=gate[:], op=MULT)

        def quantise(i, k):
            shape = [P, PASSES, len(GROUPS[k]), P]
            u_codes[i, k] = work.tile(shape, U32, name="u_codes%d" % k, tag="u_codes%d" % k, align_bytes=64)
            u_scales[i, k] = work.tile(shape, U8, name="u_scales%d" % k, tag="u_scales%d" % k, align_bytes=64)
            nc.vector.quantize_mx(
                out=u_codes[i, k][:].rearrange("p h e n -> p (h e n)").bitcast(FP8X4),
                scales=u_scales[i, k][:].rearrange("p h e n -> p (h e n)"),
                in_=u[i, k][:].rearrange("p h e n t -> p (h e n t)"),
            )

        def multiply(i, k):
            for e, d in enumerate(GROUPS[k]):
                if i == last:
                    acc[i, d] = psum_t.tile([P, C], F32, name="acc", tag="vT_ps%d" % d)
                else:
                    acc[i, d] = psum_acc.tile([P, C], F32, name="acc", tag="acc")
                for h in range(PASSES):
                    nc.tensor.matmul_mx(
                        out=acc[i, d][:],
                        lhsT=u_codes[i, k][:, h, e, :].bitcast(FP8X4),
                        lhsT_scale=u_scales[i, k][:, h, e, :],
                        rhs=wv_codes[:, h, :].bitcast(FP8X4),
                        rhs_scale=wv_scales[:, h, :],
                        start=(h == 0),
                        stop=(h == PASSES - 1),
                    )

        def residual(i, d):
            if d == 0:
                y[i] = work.tile([P, DIMS, C], F32, name="y", tag="y", bufs=3)
            nc.vector.scalar_tensor_tensor(
                out=y[i][:, d, :], in0=acc[i, d][:], scalar=1.0 / math.sqrt(PASSES * C),
                in1=v_sb[i][:, :, d], op0=MULT, op1=ADD,
            )

        def times_gain(i, first, stop):
            if first == 0:
                y_gain[i] = work.tile([P, DIMS, C], F32, name="y_gain", tag="y_gain")
            cols = scalar_cols[i]
            nc.gpsimd.tensor_tensor(
                out=y_gain[i][:, first:stop, cols], in0=y[i][:, first:stop, cols],
                in1=gain[:, cols].unsqueeze(1).to_broadcast([P, stop - first, cols.stop]), op=MULT,
            )

        def mean_square(i, first, last):
            squares = work.tile([P, DIMS, C], F32, name="squares", tag="squares")
            share = work.tile([P, 1], F32, name="share", tag="share", bufs=4)
            nc.scalar.activation(
                out=squares[:, first:last, :], in_=y[i][:, first:last, :], func=ACT.Square,
                scale=1.0 / math.sqrt(DIMS * C), accum_out=share[:],
            )
            return share

        def inverse_rms(i, share, bias):
            inv_rms[i] = work.tile([P, 1], F32, name="inv_rms", tag="inv_rms", bufs=4)
            nc.scalar.activation(out=inv_rms[i][:], in_=share[:], func=ACT.Abs_reciprocal_sqrt, bias=bias[:])

        def store(i, cols, result):
            nc.sync.dma_start(out=out[i * P : (i + 1) * P, cols, :], in_=result)

        def new_result(cols):
            tile = work.tile([P, C, DIMS], F32, name="result", tag="result", bufs=7)
            return tile[:, 0 : cols.stop - cols.start, :]

        def normalise_on_scalar(i, cols):
            result = new_result(cols)
            nc.scalar.activation(
                out=result, in_=y_gain[i][:, :, cols].rearrange("p d c -> p c d"),
                func=ACT.Copy, scale=inv_rms[i][:],
            )
            store(i, cols, result)

        def normalise_on_vector(i, cols):
            result = new_result(cols)
            nc.vector.scalar_tensor_tensor(
                out=result, in0=y[i][:, :, cols].rearrange("p d c -> p c d"), scalar=inv_rms[i][:],
                in1=gain[:, cols].unsqueeze(2).to_broadcast([P, cols.stop - cols.start, DIMS]), op0=MULT, op1=MULT,
            )
            store(i, cols, result)

        scalar_cols = {i: slice(0, 7 * C // 8) for i in range(last - 1)}
        scalar_cols[last - 1], scalar_cols[last] = slice(0, C // 2), slice(0, C // 4)
        vector_cols = {i: [slice(cols.stop, C)] for i, cols in scalar_cols.items()}
        middle = (scalar_cols[last].stop + C) // 2
        vector_cols[last] = [slice(scalar_cols[last].stop, middle), slice(middle, C)]

        second_gate(0, nc.vector, pieces=2)
        transpose_first_gate(0)
        copy_first_gate(0)
        transpose_second_gate(0)
        copy_second_gate(0)
        gather_words(0)
        for d in range(DIMS):
            turn_v(0, d)
        for i in range(1, TILES):
            second_gate(i, nc.gpsimd)

        for j in range(TILES):
            if j < last:
                transpose_first_gate(j + 1)
                transpose_second_gate(j + 1)
                if j > 0:
                    gather_words(j + 1)
                copy_first_gate(j + 1)
                copy_second_gate(j + 1)
                if j == 0:
                    gather_words(j + 1)
            if j == 0:
                group_wv(nc.scalar.copy, 0, slice(0, C))
                group_wv(nc.scalar.copy, 1, slice(0, C // 2))
            if j == 1:
                spread_gain()
            if j >= 2:
                normalise_on_scalar(j - 2, scalar_cols[j - 2])
            for d in range(DIMS):
                product(j, d, 0, g1T[j])
                product(j, d, 1, sgT[j])
                if j < last:
                    turn_v(j + 1, d)
            if j == 1:
                quantise(0, 0)
                quantise(0, 1)
                group_wv(nc.vector.tensor_copy, 1, slice(C // 2, C))
                for h in range(PASSES):
                    quantise_wv(h)
                multiply(0, 0)
                multiply(0, 1)
            if j >= 1:
                quantise(j, 0)
                quantise(j, 1)
            if j >= 2:
                for cols in vector_cols[j - 2]:
                    normalise_on_vector(j - 2, cols)
            if j >= 1:
                multiply(j, 0)
                for d in range(DIMS):
                    residual(j - 1, d)
                    if d != 1:
                        times_gain(j - 1, max(d - 1, 0), d + 1)
                multiply(j, 1)
                if j < last:
                    inverse_rms(j - 1, mean_square(j - 1, 0, DIMS), eps)

        def add_shares(first, second):
            sums = [work.tile([P, 1], F32, name="mean_sq", tag="mean_sq", bufs=4) for k in range(2)]
            nc.scalar.activation(out=sums[0][:], in_=first[:], func=ACT.Copy, bias=EPS)
            nc.scalar.activation(out=sums[1][:], in_=second[:], func=ACT.Identity, bias=sums[0][:])
            return sums[1]

        def mean_square_on_vector(i, d):
            squares = work.tile([P, C], F32, name="squares_v", tag="squares_v")
            share = work.tile([P, 1], F32, name="share_v", tag="share_v")
            nc.vector.scalar_tensor_tensor(
                out=squares[:], in0=y[i][:, d, :], scalar=1.0 / (DIMS * C), in1=y[i][:, d, :],
                op0=MULT, op1=MULT, accum_out=share[:],
            )
            return share

        for d in range(DIMS):
            residual(last, d)
            if d != 1:
                times_gain(last, max(d - 1, 0), d + 1)
        for i in (last - 1, last):
            two = add_shares(mean_square(i, 0, 1), mean_square(i, 1, 2))
            third = mean_square_on_vector(i, 2) if i == last else mean_square(i, 2, DIMS)
            inverse_rms(i, third, two)
        for i in (last - 1, last):
            normalise_on_vector(i, vector_cols[i][0])
            normalise_on_scalar(i, scalar_cols[i])
        normalise_on_vector(last, vector_cols[last][1])
